import numpy as np
import ml_dtypes


def mxq(x, axis, fmt="e4m3"):
    dtype, down = {"e4m3": (ml_dtypes.float8_e4m3fn, 7), "e5m2": (ml_dtypes.float8_e5m2, 14)}[fmt]
    v = np.moveaxis(np.asarray(x, np.float32).astype(ml_dtypes.bfloat16).astype(np.float64), axis, -1)
    blocks = v.reshape(v.shape[:-1] + (-1, 32))
    amax = np.abs(blocks).max(-1, keepdims=True)
    byte = np.maximum(np.where(amax > 0, np.frexp(amax)[1] - 1 + 127, 0) - down, 1)
    scale = np.exp2(byte - 127.0)
    codes = (blocks / scale).astype(np.float32).astype(dtype).astype(np.float64)
    return np.moveaxis((codes * scale).reshape(v.shape), -1, axis)


WIDE = False


def mx_kscale(k):
    if not WIDE:
        return np.ones(k)
    levels = np.array([10, -10, 5, -5, 0])
    a = np.random.permutation(np.resize(levels, k // 512 * 4)).reshape(k // 512, 4)
    idx = np.arange(k)
    return np.exp2(a[idx // 512, idx % 128 // 32])


BF16 = ml_dtypes.bfloat16


def bf(x):
    return np.asarray(x, np.float32).astype(BF16)


def f64(x):
    return np.asarray(x).astype(np.float64)


B, S, D, E, WINDOW = 8, 512, 1024, 512, 10
HALF = WINDOW // 2
NW = HALF + HALF + 1


def setup_inputs():
    s, t = mx_kscale(D), mx_kscale(E)
    pos = np.arange(S)[:, None] + np.arange(NW)[None, :] - HALF
    e = np.exp(np.random.standard_normal((B, S, NW))) * ((pos >= 0) & (pos < S))
    return {"x": bf(np.random.standard_normal((B, S, D)) * s),
            "Wv": bf(np.random.standard_normal((E, D)) / np.sqrt(D) / s[None, :] * t[:, None]),
            "bv": bf(np.random.standard_normal(E) * 0.1 * t),
            "attn_band": bf(e / e.sum(-1, keepdims=True)),
            "Wo": bf(np.random.standard_normal((D, E)) / np.sqrt(E) / t[None, :]),
            "bo": bf(np.random.standard_normal(D) * 0.1)}


def reference(x, Wv, bv, attn_band, Wo, bo):
    v = (mxq(f64(x), 2, "e4m3") @ mxq(f64(Wv), 1, "e4m3").T) + f64(bv)
    a = f64(attn_band)
    ctx = np.zeros((B, S, E))
    for o in range(NW):
        sh = o - HALF
        lo, hi = max(0, -sh), min(S, S - sh)
        ctx[:, lo:hi] += a[:, lo:hi, o:o + 1] * v[:, lo + sh:hi + sh]
    return (mxq(ctx, 2, "e4m3") @ mxq(f64(Wo), 1, "e4m3").T) + f64(bo)

@@ -1,0 +1,307 @@
+from contextlib import ExitStack
+
+import concourse.mybir as mybir
+from concourse.masks import make_identity
+
+F32 = mybir.dt.float32
+BF16 = mybir.dt.bfloat16
+U32 = mybir.dt.uint32
+U8 = mybir.dt.uint8
+FP8X4 = mybir.dt.float8_e4m3fn_x4
+ADD = mybir.AluOpType.add
+IS_GE = mybir.AluOpType.is_ge
+
+B, S, D, E, NW = 8, 512, 1024, 512, 11
+HALF = NW // 2
+T = B * S
+P = 128
+QUAD = 32
+PACK = 4
+K_PASS = P * PACK
+X_PASSES = D // K_PASS
+N_TILE = 512
+D_HALVES = D // N_TILE
+ROWS = S // P
+
+WIN_STEP = P - 2 * HALF
+N_WIN = -(-(T - HALF) // WIN_STEP)
+FIRST_OUT = [0] + [m * WIN_STEP + HALF for m in range(1, N_WIN)] + [T]
+MAX_OUT = WIN_STEP + HALF
+
+PER_ROUND = 2
+N_ROUNDS = -(-N_WIN // PER_ROUND)
+BAND_GROUP = 4
+LEAD = 4
+X_AHEAD = 3
+WO_ROUND = 1
+
+Z_PITCH = QUAD + NW + HALF
+SCRATCH_ROW = T - S
+
+FLOPS = 2 * T * D * E + 2 * T * NW * E + 2 * T * E * D
+
+
+def window_base(m):
+    return min(m * WIN_STEP, T - P)
+
+
+def windows_of_round(k):
+    return [m for m in range(k * PER_ROUND, (k + 1) * PER_ROUND) if 0 <= m < N_WIN]
+
+
+def tile_localattention_pb_t_kernel(tc, x, Wv, bv, attn_band, Wo, bo, out):
+    nc = tc.nc
+    x_rows = x.rearrange("b s d -> (b s) d")
+    out_rows = out.rearrange("b s d -> (b s) d")
+    scratch = out_rows[SCRATCH_ROW:T, :].rearrange("r d -> (r d)")
+
+    with ExitStack() as stack:
+        keep = stack.enter_context(tc.tile_pool(name="keep", bufs=1))
+        x_pool = stack.enter_context(tc.tile_pool(name="x_pool", bufs=PER_ROUND * (X_AHEAD + 1)))
+        q_pool = stack.enter_context(tc.tile_pool(name="q_pool", bufs=2 * PER_ROUND))
+        v_pool = stack.enter_context(tc.tile_pool(name="v_pool", bufs=PER_ROUND * (LEAD + 1)))
+        o_pool = stack.enter_context(tc.tile_pool(name="o_pool", bufs=4))
+        psum = stack.enter_context(tc.psum_pool(name="psum", bufs=PER_ROUND))
+
+        ident_f32 = keep.tile([P, P], F32)
+        ident_bf16 = keep.tile([P, P], BF16)
+        bv_all = keep.tile([P, E], BF16)
+        bo_all = keep.tile([P, D], BF16)
+        wv_raw = keep.tile([P, E // P, D], BF16)
+        wo_raw = keep.tile([P, D // P, E], BF16)
+        wv_grouped = keep.tile([P, X_PASSES, E, PACK // 2], F32, align_bytes=64)
+        wo_grouped = keep.tile([P, D, PACK], BF16, align_bytes=64)
+        wv_codes = keep.tile([P, X_PASSES, E], U32, align_bytes=64)
+        wv_scales = keep.tile([P, X_PASSES, E], U8, align_bytes=64)
+        wo_codes = keep.tile([P, D], U32, align_bytes=64)
+        wo_scales = keep.tile([P, D], U8, align_bytes=64)
+        band_raw = keep.tile([P, B, ROWS * NW], BF16)
+        band_f32 = keep.tile([P, B, ROWS, NW], F32)
+        z_rows = keep.tile([P, B, ROWS, Z_PITCH], F32)
+        band_rows = keep.tile([P, N_WIN, P], F32)
+        band_t = keep.tile([P, N_WIN, P], F32)
+        ctx_grouped = keep.tile([P, T, PACK], BF16, align_bytes=64)
+        ctx_codes = keep.tile([P, T], U32, align_bytes=64)
+        ctx_scales = keep.tile([P, T], U8, align_bytes=64)
+
+        x_tiles = {}
+        x_code_tiles = {}
+        v_tiles = {}
+
+        def load_window(m):
+            xw = x_pool.tile([P, D], BF16)
+            nc.sync.dma_start(out=xw[:], in_=x_rows[window_base(m) : window_base(m) + P, :])
+            x_tiles[m] = xw
+
+        def transpose_window(m):
+            words = x_tiles[m][:].bitcast(F32)
+            xt = psum.tile([P, X_PASSES, PACK // 2, P], F32, tag="xt")
+            for g in range(X_PASSES):
+                for u in range(PACK // 2):
+                    first = (g * (PACK // 2) + u) * P
+                    nc.tensor.transpose(xt[:, g, u, :], words[:, first : first + P], ident_f32[:])
+            xg = q_pool.tile([P, X_PASSES, P, PACK // 2], F32, align_bytes=64)
+            nc.scalar.copy(out=xg[:], in_=xt[:].rearrange("p g u t -> p g t u"))
+            return xg
+
+        def quantise_window(m, xg):
+            x_codes = q_pool.tile([P, X_PASSES, P], U32, align_bytes=64)
+            x_scales = q_pool.tile([P, X_PASSES, P], U8, align_bytes=64)
+            nc.vector.quantize_mx(
+                out=x_codes[:].rearrange("p g t -> p (g t)").bitcast(FP8X4),
+                scales=x_scales[:].rearrange("p g t -> p (g t)"),
+                in_=xg[:].rearrange("p g t u -> p (g t u)").bitcast(BF16),
+            )
+            x_code_tiles[m] = (x_codes, x_scales)
+
+        def project_values(m):
+            x_codes, x_scales = x_code_tiles[m]
+            v0 = psum.tile([P, E], F32, tag="v0")
+            for g in range(X_PASSES):
+                nc.tensor.matmul_mx(
+                    out=v0[:],
+                    lhsT=x_codes[:, g, :].bitcast(FP8X4),
+                    lhsT_scale=x_scales[:, g, :],
+                    rhs=wv_codes[:, g, :].bitcast(FP8X4),
+                    rhs_scale=wv_scales[:, g, :],
+                    start=(g == 0),
+                    stop=(g == X_PASSES - 1),
+                )
+            v = v_pool.tile([P, E], F32)
+            nc.vector.tensor_tensor(out=v[:], in0=v0[:], in1=bv_all[:], op=ADD)
+            v_tiles[m] = v
+
+        def mix_window(m):
+            first, last = FIRST_OUT[m], FIRST_OUT[m + 1]
+            width = last - first
+            col = first - window_base(m)
+            ct = psum.tile([P, PACK, MAX_OUT], F32, tag="ct")
+            for t in range(PACK):
+                nc.tensor.matmul(
+                    ct[:, t, 0:width],
+                    lhsT=v_tiles[m][:, t * P : (t + 1) * P],
+                    rhs=band_t[:, m, col : col + width],
+                    start=True,
+                    stop=True,
+                )
+            nc.scalar.copy(
+                out=ctx_grouped[:, first:last, :],
+                in_=ct[:, :, 0:width].rearrange("p t w -> p w t"),
+            )
+
+        def quantise_block(tb):
+            tokens = slice(tb * P, (tb + 1) * P)
+            nc.vector.quantize_mx(
+                out=ctx_codes[:, tokens].bitcast(FP8X4),
+                scales=ctx_scales[:, tokens],
+                in_=ctx_grouped[:, tokens, :].rearrange("p w t -> p (w t)"),
+            )
+
+        def project_block(tb):
+            tokens = slice(tb * P, (tb + 1) * P)
+            result = o_pool.tile([P, D], F32)
+            for h in range(D_HALVES):
+                cols = slice(h * N_TILE, (h + 1) * N_TILE)
+                o = psum.tile([P, N_TILE], F32, tag="o")
+                nc.tensor.matmul_mx(
+                    out=o[:],
+                    lhsT=ctx_codes[:, tokens].bitcast(FP8X4),
+                    lhsT_scale=ctx_scales[:, tokens],
+                    rhs=wo_codes[:, cols].bitcast(FP8X4),
+                    rhs_scale=wo_scales[:, cols],
+                    start=True,
+                    stop=True,
+                )
+                if h == 0:
+                    nc.vector.tensor_tensor(out=result[:, cols], in0=o[:], in1=bo_all[:, cols], op=ADD)
+                else:
+                    nc.scalar.copy(out=result[:, cols], in_=o[:])
+                    nc.gpsimd.tensor_tensor(out=result[:, cols], in0=result[:, cols], in1=bo_all[:, cols], op=ADD)
+            nc.sync.dma_start(out=out_rows[tokens, :], in_=result[:])
+
+        def prepare_wv():
+            half = E // 2
+            for g in range(X_PASSES):
+                for h in range(2):
+                    wt = psum.tile([P, PACK // 2, half], F32, tag="o")
+                    for u in range(PACK // 2):
+                        first = (g * (PACK // 2) + u) * P
+                        for c in range(half // P):
+                            words = wv_raw[:, h * (half // P) + c, :].bitcast(F32)
+                            nc.tensor.transpose(wt[:, u, c * P : (c + 1) * P], words[:, first : first + P], ident_f32[:])
+                    dst = wv_grouped[:, g, h * half : (h + 1) * half, :]
+                    if h == 0:
+                        nc.scalar.copy(out=dst, in_=wt[:].rearrange("p u e -> p e u"))
+                    else:
+                        nc.vector.tensor_copy(out=dst, in_=wt[:].rearrange("p u e -> p e u"))
+            for g in range(X_PASSES):
+                nc.vector.quantize_mx(
+                    out=wv_codes[:, g, :].bitcast(FP8X4),
+                    scales=wv_scales[:, g, :],
+                    in_=wv_grouped[:, g, :, :].rearrange("p e u -> p (e u)").bitcast(BF16),
+                )
+
+        def prepare_wo():
+            cols = 2 * P
+            for q in range(D // cols):
+                wt = psum.tile([P, PACK, cols], BF16, tag="o")
+                for t in range(PACK):
+                    for c in range(cols // P):
+                        nc.tensor.transpose(
+                            wt[:, t, c * P : (c + 1) * P],
+                            wo_raw[:, q * (cols // P) + c, t * P : (t + 1) * P],
+                            ident_bf16[:],
+                        )
+                nc.scalar.copy(
+                    out=wo_grouped[:, q * cols : (q + 1) * cols, :],
+                    in_=wt[:].rearrange("p t d -> p d t"),
+                )
+            for h in range(D_HALVES):
+                cols_h = slice(h * N_TILE, (h + 1) * N_TILE)
+                nc.vector.quantize_mx(
+                    out=wo_codes[:, cols_h].bitcast(FP8X4),
+                    scales=wo_scales[:, cols_h],
+                    in_=wo_grouped[:, cols_h, :].rearrange("p d t -> p (d t)"),
+                )
+
+        def store_band_scratch():
+            nc.vector.memset(z_rows[:], 0.0)
+            nc.vector.memset(band_rows[:], 0.0)
+            nc.vector.tensor_copy(out=band_f32[:].rearrange("p b r o -> p b (r o)"), in_=band_raw[:])
+            nc.gpsimd.affine_select(
+                out=band_f32[:], in_=band_f32[:], pattern=[[0, B], [1, ROWS], [1, NW]],
+                compare_op=IS_GE, fill=0.0, base=-HALF, channel_multiplier=ROWS,
+            )
+            nc.gpsimd.affine_select(
+                out=band_f32[:], in_=band_f32[:], pattern=[[0, B], [-1, ROWS], [-1, NW]],
+                compare_op=IS_GE, fill=0.0, base=S - 1 + HALF, channel_multiplier=-ROWS,
+            )
+            nc.vector.tensor_copy(out=z_rows[:, :, :, 0:NW], in_=band_f32[:])
+            nc.scalar.dma_start(
+                out=scratch[0 : T * Z_PITCH].rearrange("(b p x) -> p b x", b=B, p=P),
+                in_=z_rows[:].rearrange("p b r c -> p b (r c)"),
+            )
+
+        def load_band_rows(first_window, count):
+            for quad in range(P // QUAD):
+                row = quad * QUAD
+                col_lo = max(row - HALF, 0)
+                col_hi = min(row + QUAD + HALF, P)
+                start = Z_PITCH * (window_base(first_window) + row) + col_lo - row + HALF
+                src = scratch[start : start + count * Z_PITCH * WIN_STEP]
+                src = src.rearrange("(m y) -> m y", m=count)[:, 0 : QUAD * (Z_PITCH - 1)]
+                src = src.rearrange("m (r c) -> r m c", r=QUAD)[:, :, 0 : col_hi - col_lo]
+                nc.gpsimd.dma_start(
+                    out=band_rows[row : row + QUAD, first_window : first_window + count, col_lo:col_hi],
+                    in_=src,
+                )
+
+        def transpose_band_group(q):
+            group = [m for m in range(q * BAND_GROUP, (q + 1) * BAND_GROUP) if m < N_WIN]
+            bt = psum.tile([P, BAND_GROUP, P], F32, tag="ct")
+            for w, m in enumerate(group):
+                nc.tensor.transpose(bt[:, w, :], band_rows[:, m, :], ident_f32[:])
+            nc.scalar.copy(out=band_t[:, group[0] : group[0] + len(group), :], in_=bt[:, 0 : len(group), :])
+
+        nc.sync.dma_start(out=band_raw[:], in_=attn_band.rearrange("b (p r) o -> p b (r o)", p=P))
+        nc.sync.dma_start(out=wv_raw[:], in_=Wv.rearrange("(c p) k -> p c k", p=P))
+        for k in range(X_AHEAD):
+            for m in windows_of_round(k):
+                load_window(m)
+        nc.sync.dma_start(out=bv_all[:], in_=bv.partition_broadcast(P))
+        nc.sync.dma_start(out=wo_raw[:], in_=Wo.rearrange("(c p) k -> p c k", p=P))
+        nc.sync.dma_start(out=bo_all[:], in_=bo.partition_broadcast(P))
+        make_identity(nc, ident_f32[:])
+        make_identity(nc, ident_bf16[:])
+        store_band_scratch()
+        load_band_rows(0, N_WIN - 1)
+        load_band_rows(N_WIN - 1, 1)
+        prepare_wv()
+
+        blocks_done = 0
+        for it in range(N_ROUNDS + LEAD + 1):
+            mixed = min(max(it - LEAD, 0) * PER_ROUND, N_WIN)
+            blocks = list(range(blocks_done, FIRST_OUT[mixed] // P))
+            blocks_done += len(blocks)
+            for tb in blocks:
+                quantise_block(tb)
+            for m in windows_of_round(it + X_AHEAD):
+                load_window(m)
+
+            ahead = (it + 1 - LEAD) * PER_ROUND
+            if 0 <= ahead < N_WIN and ahead % BAND_GROUP == 0:
+                transpose_band_group(ahead // BAND_GROUP)
+            if it == WO_ROUND:
+                prepare_wo()
+            grouped = [(m, transpose_window(m)) for m in windows_of_round(it)]
+            for m, xg in grouped:
+                quantise_window(m, xg)
+            for m in windows_of_round(it - LEAD):
+                mix_window(m)
+
+            for tb in blocks[:1]:
+                project_block(tb)
+            for m in windows_of_round(it - 1):
+                project_values(m)
+            for tb in blocks[1:]:
+                project_block(tb)

@@ -263,6 +263,7 @@ def tile_localattention_pb_t_kernel(tc, x, Wv, bv, attn_band, Wo, bo, out):
                 nc.tensor.transpose(bt[:, w, :], band_rows[:, m, :], ident_f32[:])
             nc.scalar.copy(out=band_t[:, group[0] : group[0] + len(group), :], in_=bt[:, 0 : len(group), :])
 
+        stack.enter_context(tc.manual_schedule())
         nc.sync.dma_start(out=band_raw[:], in_=attn_band.rearrange("b (p r) o -> p b (r o)", p=P))
         nc.sync.dma_start(out=wv_raw[:], in_=Wv.rearrange("(c p) k -> p c k", p=P))
         for k in range(X_AHEAD):

@@ -10,6 +10,7 @@ U8 = mybir.dt.uint8
 FP8X4 = mybir.dt.float8_e4m3fn_x4
 ADD = mybir.AluOpType.add
 IS_GE = mybir.AluOpType.is_ge
+AXIS_X = mybir.AxisListType.X
 
 B, S, D, E, NW = 8, 512, 1024, 512, 11
 HALF = NW // 2
@@ -23,7 +24,8 @@ N_TILE = 512
 D_HALVES = D // N_TILE
 ROWS = S // P
 
-WIN_STEP = P - 2 * HALF
+TOK = P - 1
+WIN_STEP = TOK - 2 * HALF
 N_WIN = -(-(T - HALF) // WIN_STEP)
 FIRST_OUT = [0] + [m * WIN_STEP + HALF for m in range(1, N_WIN)] + [T]
 MAX_OUT = WIN_STEP + HALF
@@ -42,7 +44,7 @@ FLOPS = 2 * T * D * E + 2 * T * NW * E + 2 * T * E * D
 
 
 def window_base(m):
-    return min(m * WIN_STEP, T - P)
+    return min(m * WIN_STEP, T - TOK)
 
 
 def windows_of_round(k):
@@ -59,13 +61,12 @@ def tile_localattention_pb_t_kernel(tc, x, Wv, bv, attn_band, Wo, bo, out):
         keep = stack.enter_context(tc.tile_pool(name="keep", bufs=1))
         x_pool = stack.enter_context(tc.tile_pool(name="x_pool", bufs=PER_ROUND * (X_AHEAD + 1)))
         q_pool = stack.enter_context(tc.tile_pool(name="q_pool", bufs=2 * PER_ROUND))
-        v_pool = stack.enter_context(tc.tile_pool(name="v_pool", bufs=PER_ROUND * (LEAD + 1)))
         o_pool = stack.enter_context(tc.tile_pool(name="o_pool", bufs=4))
         psum = stack.enter_context(tc.psum_pool(name="psum", bufs=PER_ROUND))
 
         ident_f32 = keep.tile([P, P], F32)
         ident_bf16 = keep.tile([P, P], BF16)
-        bv_all = keep.tile([P, E], BF16)
+        bv_rows = keep.tile([P, E], BF16)
         bo_all = keep.tile([P, D], BF16)
         wv_raw = keep.tile([P, E // P, D], BF16)
         wo_raw = keep.tile([P, D // P, E], BF16)
@@ -78,19 +79,24 @@ def tile_localattention_pb_t_kernel(tc, x, Wv, bv, attn_band, Wo, bo, out):
         band_raw = keep.tile([P, B, ROWS * NW], BF16)
         band_f32 = keep.tile([P, B, ROWS, NW], F32)
         z_rows = keep.tile([P, B, ROWS, Z_PITCH], F32)
+        zero_rows = keep.tile([P, Z_PITCH], F32)
         band_rows = keep.tile([P, N_WIN, P], F32)
         band_t = keep.tile([P, N_WIN, P], F32)
         ctx_grouped = keep.tile([P, T, PACK], BF16, align_bytes=64)
         ctx_codes = keep.tile([P, T], U32, align_bytes=64)
         ctx_scales = keep.tile([P, T], U8, align_bytes=64)
 
+        v_tiles = [keep.tile([P, E], F32, name="v%d" % n) for n in range(PER_ROUND * (LEAD + 1))]
+
         x_tiles = {}
         x_code_tiles = {}
-        v_tiles = {}
 
         def load_window(m):
             xw = x_pool.tile([P, D], BF16)
-            nc.sync.dma_start(out=xw[:], in_=x_rows[window_base(m) : window_base(m) + P, :])
+            rows = min(P, T - window_base(m))
+            if rows < P:
+                nc.gpsimd.memset(xw[:], 0.0)
+            nc.sync.dma_start(out=xw[0:rows, :], in_=x_rows[window_base(m) : window_base(m) + rows, :])
             x_tiles[m] = xw
 
         def transpose_window(m):
@@ -127,9 +133,7 @@ def tile_localattention_pb_t_kernel(tc, x, Wv, bv, attn_band, Wo, bo, out):
                     start=(g == 0),
                     stop=(g == X_PASSES - 1),
                 )
-            v = v_pool.tile([P, E], F32)
-            nc.vector.tensor_tensor(out=v[:], in0=v0[:], in1=bv_all[:], op=ADD)
-            v_tiles[m] = v
+            nc.scalar.copy(out=v_tiles[m % len(v_tiles)][0:TOK, :], in_=v0[0:TOK, :])
 
         def mix_window(m):
             first, last = FIRST_OUT[m], FIRST_OUT[m + 1]
@@ -139,7 +143,7 @@ def tile_localattention_pb_t_kernel(tc, x, Wv, bv, attn_band, Wo, bo, out):
             for t in range(PACK):
                 nc.tensor.matmul(
                     ct[:, t, 0:width],
-                    lhsT=v_tiles[m][:, t * P : (t + 1) * P],
+                    lhsT=v_tiles[m % len(v_tiles)][:, t * P : (t + 1) * P],
                     rhs=band_t[:, m, col : col + width],
                     start=True,
                     stop=True,
@@ -172,11 +176,7 @@ def tile_localattention_pb_t_kernel(tc, x, Wv, bv, attn_band, Wo, bo, out):
                     start=True,
                     stop=True,
                 )
-                if h == 0:
-                    nc.vector.tensor_tensor(out=result[:, cols], in0=o[:], in1=bo_all[:, cols], op=ADD)
-                else:
-                    nc.scalar.copy(out=result[:, cols], in_=o[:])
-                    nc.gpsimd.tensor_tensor(out=result[:, cols], in0=result[:, cols], in1=bo_all[:, cols], op=ADD)
+                nc.vector.tensor_tensor(out=result[:, cols], in0=o[:], in1=bo_all[:, cols], op=ADD)
             nc.sync.dma_start(out=out_rows[tokens, :], in_=result[:])
 
         def prepare_wv():
@@ -226,6 +226,7 @@ def tile_localattention_pb_t_kernel(tc, x, Wv, bv, attn_band, Wo, bo, out):
 
         def store_band_scratch():
             nc.vector.memset(z_rows[:], 0.0)
+            nc.vector.memset(zero_rows[:], 0.0)
             nc.vector.memset(band_rows[:], 0.0)
             nc.vector.tensor_copy(out=band_f32[:].rearrange("p b r o -> p b (r o)"), in_=band_raw[:])
             nc.gpsimd.affine_select(
@@ -241,12 +242,16 @@ def tile_localattention_pb_t_kernel(tc, x, Wv, bv, attn_band, Wo, bo, out):
                 out=scratch[0 : T * Z_PITCH].rearrange("(b p x) -> p b x", b=B, p=P),
                 in_=z_rows[:].rearrange("p b r c -> p b (r c)"),
             )
+            nc.scalar.dma_start(
+                out=scratch[T * Z_PITCH : (T + P) * Z_PITCH].rearrange("(p c) -> p c", p=P),
+                in_=zero_rows[:],
+            )
 
         def load_band_rows(first_window, count):
             for quad in range(P // QUAD):
                 row = quad * QUAD
                 col_lo = max(row - HALF, 0)
-                col_hi = min(row + QUAD + HALF, P)
+                col_hi = min(row + QUAD + HALF, TOK)
                 start = Z_PITCH * (window_base(first_window) + row) + col_lo - row + HALF
                 src = scratch[start : start + count * Z_PITCH * WIN_STEP]
                 src = src.rearrange("(m y) -> m y", m=count)[:, 0 : QUAD * (Z_PITCH - 1)]
@@ -258,18 +263,21 @@ def tile_localattention_pb_t_kernel(tc, x, Wv, bv, attn_band, Wo, bo, out):
 
         def transpose_band_group(q):
             group = [m for m in range(q * BAND_GROUP, (q + 1) * BAND_GROUP) if m < N_WIN]
+            members = slice(group[0], group[0] + len(group))
+            nc.vector.tensor_reduce(
+                out=band_rows[:, members, TOK:P], in_=band_rows[:, members, 0:TOK], axis=AXIS_X, op=ADD
+            )
             bt = psum.tile([P, BAND_GROUP, P], F32, tag="ct")
             for w, m in enumerate(group):
                 nc.tensor.transpose(bt[:, w, :], band_rows[:, m, :], ident_f32[:])
-            nc.scalar.copy(out=band_t[:, group[0] : group[0] + len(group), :], in_=bt[:, 0 : len(group), :])
+            nc.scalar.copy(out=band_t[:, members, :], in_=bt[:, 0 : len(group), :])
 
-        stack.enter_context(tc.manual_schedule())
         nc.sync.dma_start(out=band_raw[:], in_=attn_band.rearrange("b (p r) o -> p b (r o)", p=P))
         nc.sync.dma_start(out=wv_raw[:], in_=Wv.rearrange("(c p) k -> p c k", p=P))
         for k in range(X_AHEAD):
             for m in windows_of_round(k):
                 load_window(m)
-        nc.sync.dma_start(out=bv_all[:], in_=bv.partition_broadcast(P))
+        nc.sync.dma_start(out=bv_rows[P - QUAD : P, :], in_=bv.partition_broadcast(QUAD))
         nc.sync.dma_start(out=wo_raw[:], in_=Wo.rearrange("(c p) k -> p c k", p=P))
         nc.sync.dma_start(out=bo_all[:], in_=bo.partition_broadcast(P))
         make_identity(nc, ident_f32[:])
@@ -277,6 +285,8 @@ def tile_localattention_pb_t_kernel(tc, x, Wv, bv, attn_band, Wo, bo, out):
         store_band_scratch()
         load_band_rows(0, N_WIN - 1)
         load_band_rows(N_WIN - 1, 1)
+        for v in v_tiles:
+            nc.vector.tensor_copy(out=v[P - QUAD : P, :], in_=bv_rows[P - QUAD : P, :])
         prepare_wv()
 
         blocks_done = 0

@@ -9,6 +9,9 @@ U32 = mybir.dt.uint32
 U8 = mybir.dt.uint8
 FP8X4 = mybir.dt.float8_e4m3fn_x4
 ADD = mybir.AluOpType.add
+MULT = mybir.AluOpType.mult
+MIN = mybir.AluOpType.min
+NOT_EQUAL = mybir.AluOpType.not_equal
 IS_GE = mybir.AluOpType.is_ge
 AXIS_X = mybir.AxisListType.X
 
@@ -20,9 +23,14 @@ QUAD = 32
 PACK = 4
 K_PASS = P * PACK
 X_PASSES = D // K_PASS
+PAIRS = PACK // 2
+N_QUAD = P // QUAD
+K_QUAD = D // N_QUAD
+K_BLOCKS = K_QUAD // 2 // QUAD
 N_TILE = 512
 D_HALVES = D // N_TILE
-ROWS = S // P
+ROWS = T // P
+PARTS = P // B
 
 TOK = P - 1
 WIN_STEP = TOK - 2 * HALF
@@ -30,25 +38,21 @@ N_WIN = -(-(T - HALF) // WIN_STEP)
 FIRST_OUT = [0] + [m * WIN_STEP + HALF for m in range(1, N_WIN)] + [T]
 MAX_OUT = WIN_STEP + HALF
 
-PER_ROUND = 2
-N_ROUNDS = -(-N_WIN // PER_ROUND)
-BAND_GROUP = 4
-LEAD = 4
-X_AHEAD = 3
-WO_ROUND = 1
+LEAD = 3
+X_AHEAD = 6
+N_V = LEAD + 3
+WO_PARTS = 4
 
 Z_PITCH = QUAD + NW + HALF
 SCRATCH_ROW = T - S
+Z_START = T
+Z_END = Z_START + T * Z_PITCH
 
 FLOPS = 2 * T * D * E + 2 * T * NW * E + 2 * T * E * D
 
 
 def window_base(m):
-    return min(m * WIN_STEP, T - TOK)
-
-
-def windows_of_round(k):
-    return [m for m in range(k * PER_ROUND, (k + 1) * PER_ROUND) if 0 <= m < N_WIN]
+    return m * WIN_STEP
 
 
 def tile_localattention_pb_t_kernel(tc, x, Wv, bv, attn_band, Wo, bo, out):
@@ -59,55 +63,78 @@ def tile_localattention_pb_t_kernel(tc, x, Wv, bv, attn_band, Wo, bo, out):
 
     with ExitStack() as stack:
         keep = stack.enter_context(tc.tile_pool(name="keep", bufs=1))
-        x_pool = stack.enter_context(tc.tile_pool(name="x_pool", bufs=PER_ROUND * (X_AHEAD + 1)))
-        q_pool = stack.enter_context(tc.tile_pool(name="q_pool", bufs=2 * PER_ROUND))
+        x_pool = stack.enter_context(tc.tile_pool(name="x_pool", bufs=X_AHEAD + 2))
+        q_pool = stack.enter_context(tc.tile_pool(name="q_pool", bufs=3))
         o_pool = stack.enter_context(tc.tile_pool(name="o_pool", bufs=4))
-        psum = stack.enter_context(tc.psum_pool(name="psum", bufs=PER_ROUND))
+        psum = stack.enter_context(tc.psum_pool(name="psum", bufs=2))
+        out_psum = stack.enter_context(tc.psum_pool(name="out_psum", bufs=2 * D_HALVES))
 
-        ident_f32 = keep.tile([P, P], F32)
         ident_bf16 = keep.tile([P, P], BF16)
         bv_rows = keep.tile([P, E], BF16)
         bo_all = keep.tile([P, D], BF16)
-        wv_raw = keep.tile([P, E // P, D], BF16)
+        wv_raw = keep.tile([P, E // QUAD, K_QUAD], BF16, align_bytes=64)
+        wv_flipped = keep.tile([P, E // QUAD, K_BLOCKS, QUAD], F32, align_bytes=64)
         wo_raw = keep.tile([P, D // P, E], BF16)
-        wv_grouped = keep.tile([P, X_PASSES, E, PACK // 2], F32, align_bytes=64)
+        wv_grouped = keep.tile([P, X_PASSES, E, PAIRS], F32, align_bytes=64)
         wo_grouped = keep.tile([P, D, PACK], BF16, align_bytes=64)
         wv_codes = keep.tile([P, X_PASSES, E], U32, align_bytes=64)
         wv_scales = keep.tile([P, X_PASSES, E], U8, align_bytes=64)
         wo_codes = keep.tile([P, D], U32, align_bytes=64)
         wo_scales = keep.tile([P, D], U8, align_bytes=64)
-        band_raw = keep.tile([P, B, ROWS * NW], BF16)
-        band_f32 = keep.tile([P, B, ROWS, NW], F32)
-        z_rows = keep.tile([P, B, ROWS, Z_PITCH], F32)
+        band_raw = keep.tile([P, ROWS, NW], BF16)
+        before_raw = keep.tile([P, HALF, NW], BF16)
+        after_raw = keep.tile([P, HALF, NW], BF16)
+        band_f32 = keep.tile([P, HALF + ROWS + HALF, NW], F32)
+        not_first = keep.tile([P, B], F32)
+        not_last = keep.tile([P, B], F32)
+        not_first_part = keep.tile([P, 1], F32)
+        not_last_part = keep.tile([P, 1], F32)
+        first_mask = keep.tile([P, HALF, NW], F32)
+        last_mask = keep.tile([P, HALF, NW], F32)
+        weight_sums = keep.tile([P, ROWS], F32)
+        z_rows = keep.tile([P, ROWS, Z_PITCH], F32)
         zero_rows = keep.tile([P, Z_PITCH], F32)
-        band_rows = keep.tile([P, N_WIN, P], F32)
         band_t = keep.tile([P, N_WIN, P], F32)
         ctx_grouped = keep.tile([P, T, PACK], BF16, align_bytes=64)
         ctx_codes = keep.tile([P, T], U32, align_bytes=64)
         ctx_scales = keep.tile([P, T], U8, align_bytes=64)
 
-        v_tiles = [keep.tile([P, E], F32, name="v%d" % n) for n in range(PER_ROUND * (LEAD + 1))]
+        v_tiles = [keep.tile([P, E], F32, name="v%d" % n) for n in range(N_V)]
 
         x_tiles = {}
         x_code_tiles = {}
 
         def load_window(m):
-            xw = x_pool.tile([P, D], BF16)
+            xw = x_pool.tile([P, P // QUAD, K_QUAD], BF16, align_bytes=64)
             rows = min(P, T - window_base(m))
             if rows < P:
                 nc.gpsimd.memset(xw[:], 0.0)
-            nc.sync.dma_start(out=xw[0:rows, :], in_=x_rows[window_base(m) : window_base(m) + rows, :])
+            full, part = divmod(rows, QUAD)
+            for a in range(N_QUAD):
+                quad = slice(a * QUAD, (a + 1) * QUAD)
+                src = x_rows[window_base(m) : window_base(m) + full * QUAD, a * K_QUAD : (a + 1) * K_QUAD]
+                nc.sync.dma_start(out=xw[quad, 0:full, :], in_=src.rearrange("(b j) k -> j b k", j=QUAD))
+                if part:
+                    first = window_base(m) + full * QUAD
+                    src = x_rows[first : first + part, a * K_QUAD : (a + 1) * K_QUAD]
+                    nc.sync.dma_start(out=xw[a * QUAD : a * QUAD + part, full, :], in_=src)
             x_tiles[m] = xw
 
         def transpose_window(m):
-            words = x_tiles[m][:].bitcast(F32)
-            xt = psum.tile([P, X_PASSES, PACK // 2, P], F32, tag="xt")
+            flipped = q_pool.tile([P, P // QUAD, K_BLOCKS, QUAD], F32, align_bytes=64)
+            nc.vector.transpose(
+                out=flipped[:].rearrange("p b w j -> p (b w j)"),
+                in_=x_tiles[m][:].rearrange("p b k -> p (b k)").bitcast(F32),
+            )
+            return flipped
+
+        def group_window(m, flipped):
+            xg = q_pool.tile([P, X_PASSES, P, PAIRS], F32, align_bytes=64)
             for g in range(X_PASSES):
-                for u in range(PACK // 2):
-                    first = (g * (PACK // 2) + u) * P
-                    nc.tensor.transpose(xt[:, g, u, :], words[:, first : first + P], ident_f32[:])
-            xg = q_pool.tile([P, X_PASSES, P, PACK // 2], F32, align_bytes=64)
-            nc.scalar.copy(out=xg[:], in_=xt[:].rearrange("p g u t -> p g t u"))
+                nc.scalar.copy(
+                    out=xg[:, g, :, :].rearrange("p (b j) u -> p b j u", j=QUAD),
+                    in_=flipped[:, :, g : K_BLOCKS : X_PASSES, :].rearrange("p b u j -> p b j u"),
+                )
             return xg
 
         def quantise_window(m, xg):
@@ -133,7 +160,10 @@ def tile_localattention_pb_t_kernel(tc, x, Wv, bv, attn_band, Wo, bo, out):
                     start=(g == 0),
                     stop=(g == X_PASSES - 1),
                 )
-            nc.scalar.copy(out=v_tiles[m % len(v_tiles)][0:TOK, :], in_=v0[0:TOK, :])
+            return v0
+
+        def keep_values(m, v0):
+            nc.scalar.copy(out=v_tiles[m % N_V][0:TOK, :], in_=v0[0:TOK, :])
 
         def mix_window(m):
             first, last = FIRST_OUT[m], FIRST_OUT[m + 1]
@@ -143,11 +173,16 @@ def tile_localattention_pb_t_kernel(tc, x, Wv, bv, attn_band, Wo, bo, out):
             for t in range(PACK):
                 nc.tensor.matmul(
                     ct[:, t, 0:width],
-                    lhsT=v_tiles[m % len(v_tiles)][:, t * P : (t + 1) * P],
+                    lhsT=v_tiles[m % N_V][:, t * P : (t + 1) * P],
                     rhs=band_t[:, m, col : col + width],
                     start=True,
                     stop=True,
                 )
+            return ct
+
+        def keep_context(m, ct):
+            first, last = FIRST_OUT[m], FIRST_OUT[m + 1]
+            width = last - first
             nc.scalar.copy(
                 out=ctx_grouped[:, first:last, :],
                 in_=ct[:, :, 0:width].rearrange("p t w -> p w t"),
@@ -163,10 +198,10 @@ def tile_localattention_pb_t_kernel(tc, x, Wv, bv, attn_band, Wo, bo, out):
 
         def project_block(tb):
             tokens = slice(tb * P, (tb + 1) * P)
-            result = o_pool.tile([P, D], F32)
+            halves = []
             for h in range(D_HALVES):
                 cols = slice(h * N_TILE, (h + 1) * N_TILE)
-                o = psum.tile([P, N_TILE], F32, tag="o")
+                o = out_psum.tile([P, N_TILE], F32, tag="o")
                 nc.tensor.matmul_mx(
                     out=o[:],
                     lhsT=ctx_codes[:, tokens].bitcast(FP8X4),
@@ -176,24 +211,25 @@ def tile_localattention_pb_t_kernel(tc, x, Wv, bv, attn_band, Wo, bo, out):
                     start=True,
                     stop=True,
                 )
-                nc.vector.tensor_tensor(out=result[:, cols], in0=o[:], in1=bo_all[:, cols], op=ADD)
-            nc.sync.dma_start(out=out_rows[tokens, :], in_=result[:])
+                halves.append(o)
+            return halves
+
+        def add_bias(result, halves, h):
+            cols = slice(h * N_TILE, (h + 1) * N_TILE)
+            nc.vector.tensor_tensor(out=result[:, cols], in0=halves[h][:], in1=bo_all[:, cols], op=ADD)
 
         def prepare_wv():
-            half = E // 2
+            nc.vector.transpose(
+                out=wv_flipped[:].rearrange("p b w j -> p (b w j)"),
+                in_=wv_raw[:].rearrange("p b k -> p (b k)").bitcast(F32),
+            )
             for g in range(X_PASSES):
-                for h in range(2):
-                    wt = psum.tile([P, PACK // 2, half], F32, tag="o")
-                    for u in range(PACK // 2):
-                        first = (g * (PACK // 2) + u) * P
-                        for c in range(half // P):
-                            words = wv_raw[:, h * (half // P) + c, :].bitcast(F32)
-                            nc.tensor.transpose(wt[:, u, c * P : (c + 1) * P], words[:, first : first + P], ident_f32[:])
-                    dst = wv_grouped[:, g, h * half : (h + 1) * half, :]
-                    if h == 0:
-                        nc.scalar.copy(out=dst, in_=wt[:].rearrange("p u e -> p e u"))
-                    else:
-                        nc.vector.tensor_copy(out=dst, in_=wt[:].rearrange("p u e -> p e u"))
+                dst = wv_grouped[:, g, :, :].rearrange("p (b j) u -> p b j u", j=QUAD)
+                src = wv_flipped[:, :, g : K_BLOCKS : X_PASSES, :].rearrange("p b u j -> p b j u")
+                if g == 0:
+                    nc.scalar.copy(out=dst, in_=src)
+                else:
+                    nc.vector.tensor_copy(out=dst, in_=src)
             for g in range(X_PASSES):
                 nc.vector.quantize_mx(
                     out=wv_codes[:, g, :].bitcast(FP8X4),
@@ -201,118 +237,160 @@ def tile_localattention_pb_t_kernel(tc, x, Wv, bv, attn_band, Wo, bo, out):
                     in_=wv_grouped[:, g, :, :].rearrange("p e u -> p (e u)").bitcast(BF16),
                 )
 
-        def prepare_wo():
-            cols = 2 * P
-            for q in range(D // cols):
-                wt = psum.tile([P, PACK, cols], BF16, tag="o")
-                for t in range(PACK):
-                    for c in range(cols // P):
-                        nc.tensor.transpose(
-                            wt[:, t, c * P : (c + 1) * P],
-                            wo_raw[:, q * (cols // P) + c, t * P : (t + 1) * P],
-                            ident_bf16[:],
-                        )
-                nc.scalar.copy(
-                    out=wo_grouped[:, q * cols : (q + 1) * cols, :],
-                    in_=wt[:].rearrange("p t d -> p d t"),
+        def prepare_wo(q):
+            cols = D // WO_PARTS
+            wt = out_psum.tile([P, PACK, cols], BF16, tag="o")
+            for t in range(PACK):
+                for c in range(cols // P):
+                    nc.tensor.transpose(
+                        wt[:, t, c * P : (c + 1) * P],
+                        wo_raw[:, q * (cols // P) + c, t * P : (t + 1) * P],
+                        ident_bf16[:],
+                    )
+            dst = wo_grouped[:, q * cols : (q + 1) * cols, :]
+            if q % 2 == 0:
+                nc.scalar.copy(out=dst, in_=wt[:].rearrange("p t d -> p d t"))
+            else:
+                nc.vector.tensor_copy(out=dst, in_=wt[:].rearrange("p t d -> p d t"))
+
+        def quantise_wo(h):
+            cols = slice(h * N_TILE, (h + 1) * N_TILE)
+            nc.vector.quantize_mx(
+                out=wo_codes[:, cols].bitcast(FP8X4),
+                scales=wo_scales[:, cols],
+                in_=wo_grouped[:, cols, :].rearrange("p d t -> p (d t)"),
+            )
+
+        def make_masks():
+            for tile, part, edge in ((not_first, not_first_part, 0), (not_last, not_last_part, PARTS - 1)):
+                nc.gpsimd.memset(tile[:], 1.0)
+                nc.gpsimd.affine_select(
+                    out=tile[:], in_=tile[:], pattern=[[-PARTS, B]],
+                    compare_op=NOT_EQUAL, fill=0.0, base=-edge, channel_multiplier=1,
                 )
-            for h in range(D_HALVES):
-                cols_h = slice(h * N_TILE, (h + 1) * N_TILE)
-                nc.vector.quantize_mx(
-                    out=wo_codes[:, cols_h].bitcast(FP8X4),
-                    scales=wo_scales[:, cols_h],
-                    in_=wo_grouped[:, cols_h, :].rearrange("p d t -> p (d t)"),
-                )
+                nc.vector.tensor_reduce(out=part[:], in_=tile[:], axis=AXIS_X, op=MIN)
+            nc.gpsimd.memset(first_mask[:], 1.0)
+            nc.gpsimd.affine_select(
+                out=first_mask[:], in_=first_mask[:], pattern=[[1, HALF], [1, NW]],
+                compare_op=IS_GE, fill=0.0, base=-HALF, channel_multiplier=0,
+            )
+            nc.gpsimd.memset(last_mask[:], 1.0)
+            nc.gpsimd.affine_select(
+                out=last_mask[:], in_=last_mask[:], pattern=[[-1, HALF], [-1, NW]],
+                compare_op=IS_GE, fill=0.0, base=2 * HALF - 1, channel_multiplier=0,
+            )
+            nc.vector.tensor_scalar_max(out=first_mask[:], in0=first_mask[:], scalar1=not_first_part[:])
+            nc.vector.tensor_scalar_max(out=last_mask[:], in0=last_mask[:], scalar1=not_last_part[:])
 
         def store_band_scratch():
-            nc.vector.memset(z_rows[:], 0.0)
-            nc.vector.memset(zero_rows[:], 0.0)
-            nc.vector.memset(band_rows[:], 0.0)
-            nc.vector.tensor_copy(out=band_f32[:].rearrange("p b r o -> p b (r o)"), in_=band_raw[:])
-            nc.gpsimd.affine_select(
-                out=band_f32[:], in_=band_f32[:], pattern=[[0, B], [1, ROWS], [1, NW]],
-                compare_op=IS_GE, fill=0.0, base=-HALF, channel_multiplier=ROWS,
+            nc.vector.tensor_scalar_mul(out=band_f32[:, 0:HALF, :], in0=before_raw[:], scalar1=not_first_part[:])
+            nc.vector.tensor_scalar_mul(
+                out=band_f32[:, HALF + ROWS : HALF + ROWS + HALF, :], in0=after_raw[:], scalar1=not_last_part[:]
             )
-            nc.gpsimd.affine_select(
-                out=band_f32[:], in_=band_f32[:], pattern=[[0, B], [-1, ROWS], [-1, NW]],
-                compare_op=IS_GE, fill=0.0, base=S - 1 + HALF, channel_multiplier=-ROWS,
+            own = band_f32[:, HALF : HALF + ROWS, :]
+            nc.scalar.copy(out=own[:, HALF : ROWS - HALF, :], in_=band_raw[:, HALF : ROWS - HALF, :])
+            nc.vector.tensor_tensor(out=own[:, 0:HALF, :], in0=band_raw[:, 0:HALF, :], in1=first_mask[:], op=MULT)
+            nc.vector.tensor_tensor(
+                out=own[:, ROWS - HALF : ROWS, :], in0=band_raw[:, ROWS - HALF : ROWS, :], in1=last_mask[:], op=MULT
             )
-            nc.vector.tensor_copy(out=z_rows[:, :, :, 0:NW], in_=band_f32[:])
+            for d in range(NW):
+                nc.vector.tensor_copy(
+                    out=z_rows[:, :, d : d + 1], in_=band_f32[:, d : d + ROWS, NW - 1 - d : NW - d]
+                )
             nc.scalar.dma_start(
-                out=scratch[0 : T * Z_PITCH].rearrange("(b p x) -> p b x", b=B, p=P),
-                in_=z_rows[:].rearrange("p b r c -> p b (r c)"),
+                out=scratch[Z_START:Z_END].rearrange("(p x) -> p x", p=P),
+                in_=z_rows[:].rearrange("p r c -> p (r c)"),
             )
             nc.scalar.dma_start(
-                out=scratch[T * Z_PITCH : (T + P) * Z_PITCH].rearrange("(p c) -> p c", p=P),
+                out=scratch[Z_END : Z_END + P * Z_PITCH].rearrange("(p c) -> p c", p=P),
                 in_=zero_rows[:],
             )
+            nc.vector.tensor_reduce(out=weight_sums[:], in_=own, axis=AXIS_X, op=ADD)
+            nc.scalar.dma_start(
+                out=scratch[0:T].rearrange("(p r) -> p r", p=P), in_=weight_sums[:]
+            )
 
-        def load_band_rows(first_window, count):
+        def load_band():
             for quad in range(P // QUAD):
                 row = quad * QUAD
                 col_lo = max(row - HALF, 0)
                 col_hi = min(row + QUAD + HALF, TOK)
-                start = Z_PITCH * (window_base(first_window) + row) + col_lo - row + HALF
-                src = scratch[start : start + count * Z_PITCH * WIN_STEP]
-                src = src.rearrange("(m y) -> m y", m=count)[:, 0 : QUAD * (Z_PITCH - 1)]
+                start = Z_START + Z_PITCH * row + col_lo - row + HALF
+                src = scratch[start : start + N_WIN * Z_PITCH * WIN_STEP]
+                src = src.rearrange("(m y) -> m y", m=N_WIN)[:, 0 : QUAD * (Z_PITCH - 1)]
                 src = src.rearrange("m (r c) -> r m c", r=QUAD)[:, :, 0 : col_hi - col_lo]
-                nc.gpsimd.dma_start(
-                    out=band_rows[row : row + QUAD, first_window : first_window + count, col_lo:col_hi],
-                    in_=src,
-                )
+                nc.sync.dma_start(out=band_t[row : row + QUAD, :, col_lo:col_hi], in_=src)
+            first = scratch[0:MAX_OUT].rearrange("(o y) -> o y", o=1)
+            nc.sync.dma_start(out=band_t[TOK:P, 0, 0:MAX_OUT], in_=first)
+            others = scratch[MAX_OUT : MAX_OUT + (N_WIN - 1) * WIN_STEP]
+            others = others.rearrange("(o m y) -> o m y", o=1, m=N_WIN - 1)
+            nc.sync.dma_start(out=band_t[TOK:P, 1:N_WIN, HALF:MAX_OUT], in_=others)
 
-        def transpose_band_group(q):
-            group = [m for m in range(q * BAND_GROUP, (q + 1) * BAND_GROUP) if m < N_WIN]
-            members = slice(group[0], group[0] + len(group))
-            nc.vector.tensor_reduce(
-                out=band_rows[:, members, TOK:P], in_=band_rows[:, members, 0:TOK], axis=AXIS_X, op=ADD
+        stack.enter_context(tc.manual_schedule())
+        weights = attn_band.rearrange("b s o -> (b s o)").rearrange("(p r o) -> p r o", p=P, o=NW)
+        nc.vector.memset(before_raw[:], 0.0)
+        nc.vector.memset(after_raw[:], 0.0)
+        nc.sync.dma_start(out=band_raw[:], in_=weights)
+        nc.sync.dma_start(out=before_raw[1:P, :, :], in_=weights[0 : P - 1, ROWS - HALF : ROWS, :])
+        nc.sync.dma_start(out=after_raw[0 : P - 1, :, :], in_=weights[1:P, 0:HALF, :])
+        for a in range(N_QUAD):
+            nc.sync.dma_start(
+                out=wv_raw[a * QUAD : (a + 1) * QUAD, :, :],
+                in_=Wv[:, a * K_QUAD : (a + 1) * K_QUAD].rearrange("(b j) k -> j b k", j=QUAD),
             )
-            bt = psum.tile([P, BAND_GROUP, P], F32, tag="ct")
-            for w, m in enumerate(group):
-                nc.tensor.transpose(bt[:, w, :], band_rows[:, m, :], ident_f32[:])
-            nc.scalar.copy(out=band_t[:, members, :], in_=bt[:, 0 : len(group), :])
-
-        nc.sync.dma_start(out=band_raw[:], in_=attn_band.rearrange("b (p r) o -> p b (r o)", p=P))
-        nc.sync.dma_start(out=wv_raw[:], in_=Wv.rearrange("(c p) k -> p c k", p=P))
-        for k in range(X_AHEAD):
-            for m in windows_of_round(k):
-                load_window(m)
+        for m in range(2):
+            load_window(m)
         nc.sync.dma_start(out=bv_rows[P - QUAD : P, :], in_=bv.partition_broadcast(QUAD))
         nc.sync.dma_start(out=wo_raw[:], in_=Wo.rearrange("(c p) k -> p c k", p=P))
+        for m in range(2, X_AHEAD):
+            load_window(m)
         nc.sync.dma_start(out=bo_all[:], in_=bo.partition_broadcast(P))
-        make_identity(nc, ident_f32[:])
+        nc.vector.memset(zero_rows[:], 0.0)
+        nc.vector.memset(z_rows[:], 0.0)
+        make_masks()
         make_identity(nc, ident_bf16[:])
+        nc.gpsimd.memset(band_t[:], 0.0)
         store_band_scratch()
-        load_band_rows(0, N_WIN - 1)
-        load_band_rows(N_WIN - 1, 1)
-        for v in v_tiles:
-            nc.vector.tensor_copy(out=v[P - QUAD : P, :], in_=bv_rows[P - QUAD : P, :])
+        load_band()
         prepare_wv()
 
+        previous = []
         blocks_done = 0
-        for it in range(N_ROUNDS + LEAD + 1):
-            mixed = min(max(it - LEAD, 0) * PER_ROUND, N_WIN)
+        grouped = flipped = None
+        for step in range(N_WIN + LEAD + 4):
+            mixing = step - 2 - LEAD
+            mixed = min(max(mixing, 0), N_WIN)
             blocks = list(range(blocks_done, FIRST_OUT[mixed] // P))
             blocks_done += len(blocks)
+            if step + X_AHEAD < N_WIN:
+                load_window(step + X_AHEAD)
             for tb in blocks:
                 quantise_block(tb)
-            for m in windows_of_round(it + X_AHEAD):
-                load_window(m)
-
-            ahead = (it + 1 - LEAD) * PER_ROUND
-            if 0 <= ahead < N_WIN and ahead % BAND_GROUP == 0:
-                transpose_band_group(ahead // BAND_GROUP)
-            if it == WO_ROUND:
-                prepare_wo()
-            grouped = [(m, transpose_window(m)) for m in windows_of_round(it)]
-            for m, xg in grouped:
-                quantise_window(m, xg)
-            for m in windows_of_round(it - LEAD):
-                mix_window(m)
-
-            for tb in blocks[:1]:
-                project_block(tb)
-            for m in windows_of_round(it - 1):
-                project_values(m)
-            for tb in blocks[1:]:
-                project_block(tb)
+            ct = mix_window(mixing) if 0 <= mixing < N_WIN else None
+            if 0 <= step - 1 < N_WIN:
+                grouped = group_window(step - 1, flipped)
+            v0 = project_values(step - 2) if 0 <= step - 2 < N_WIN else None
+            if ct is not None:
+                keep_context(mixing, ct)
+            if v0 is not None:
+                keep_values(step - 2, v0)
+            projected = [(tb, project_block(tb)) for tb in blocks]
+            results = []
+            for tb, halves in previous:
+                result = o_pool.tile([P, D], F32)
+                add_bias(result, halves, 0)
+                results.append(result)
+            if step < N_WIN:
+                flipped = transpose_window(step)
+            for (tb, halves), result in zip(previous, results):
+                add_bias(result, halves, 1)
+                nc.sync.dma_start(out=out_rows[tb * P : (tb + 1) * P, :], in_=result[:])
+            if 0 <= step - 1 < N_WIN:
+                quantise_window(step - 1, grouped)
+            previous = projected
+            if step < WO_PARTS:
+                prepare_wo(step)
+            if WO_PARTS <= step < WO_PARTS + D_HALVES:
+                quantise_wo(step - WO_PARTS)
+            if step < N_V:
+                nc.vector.tensor_copy(out=v_tiles[step][P - QUAD : P, :], in_=bv_rows[P - QUAD : P, :])

@@ -24,9 +24,6 @@ PACK = 4
 K_PASS = P * PACK
 X_PASSES = D // K_PASS
 PAIRS = PACK // 2
-N_QUAD = P // QUAD
-K_QUAD = D // N_QUAD
-K_BLOCKS = K_QUAD // 2 // QUAD
 N_TILE = 512
 D_HALVES = D // N_TILE
 ROWS = T // P
@@ -42,8 +39,11 @@ LEAD = 3
 X_AHEAD = 6
 N_V = LEAD + 3
 WO_PARTS = 4
+WO_FIRST = 1
 
 Z_PITCH = QUAD + NW + HALF
+BAND_ROWS = ((0, QUAD), (QUAD, QUAD), (2 * QUAD, QUAD), (3 * QUAD, QUAD // 2), (3 * QUAD + QUAD // 2, QUAD // 2 - 1))
+BAND_FIRST = 8
 SCRATCH_ROW = T - S
 Z_START = T
 Z_END = Z_START + T * Z_PITCH
@@ -67,13 +67,12 @@ def tile_localattention_pb_t_kernel(tc, x, Wv, bv, attn_band, Wo, bo, out):
         q_pool = stack.enter_context(tc.tile_pool(name="q_pool", bufs=3))
         o_pool = stack.enter_context(tc.tile_pool(name="o_pool", bufs=4))
         psum = stack.enter_context(tc.psum_pool(name="psum", bufs=2))
-        out_psum = stack.enter_context(tc.psum_pool(name="out_psum", bufs=2 * D_HALVES))
 
+        ident_f32 = keep.tile([P, P], F32)
         ident_bf16 = keep.tile([P, P], BF16)
         bv_rows = keep.tile([P, E], BF16)
         bo_all = keep.tile([P, D], BF16)
-        wv_raw = keep.tile([P, E // QUAD, K_QUAD], BF16, align_bytes=64)
-        wv_flipped = keep.tile([P, E // QUAD, K_BLOCKS, QUAD], F32, align_bytes=64)
+        wv_raw = keep.tile([P, E // P, D], BF16)
         wo_raw = keep.tile([P, D // P, E], BF16)
         wv_grouped = keep.tile([P, X_PASSES, E, PAIRS], F32, align_bytes=64)
         wo_grouped = keep.tile([P, D, PACK], BF16, align_bytes=64)
@@ -105,36 +104,25 @@ def tile_localattention_pb_t_kernel(tc, x, Wv, bv, attn_band, Wo, bo, out):
         x_code_tiles = {}
 
         def load_window(m):
-            xw = x_pool.tile([P, P // QUAD, K_QUAD], BF16, align_bytes=64)
+            xw = x_pool.tile([P, D], BF16)
             rows = min(P, T - window_base(m))
             if rows < P:
                 nc.gpsimd.memset(xw[:], 0.0)
-            full, part = divmod(rows, QUAD)
-            for a in range(N_QUAD):
-                quad = slice(a * QUAD, (a + 1) * QUAD)
-                src = x_rows[window_base(m) : window_base(m) + full * QUAD, a * K_QUAD : (a + 1) * K_QUAD]
-                nc.sync.dma_start(out=xw[quad, 0:full, :], in_=src.rearrange("(b j) k -> j b k", j=QUAD))
-                if part:
-                    first = window_base(m) + full * QUAD
-                    src = x_rows[first : first + part, a * K_QUAD : (a + 1) * K_QUAD]
-                    nc.sync.dma_start(out=xw[a * QUAD : a * QUAD + part, full, :], in_=src)
+            nc.sync.dma_start(out=xw[0:rows, :], in_=x_rows[window_base(m) : window_base(m) + rows, :])
             x_tiles[m] = xw
 
         def transpose_window(m):
-            flipped = q_pool.tile([P, P // QUAD, K_BLOCKS, QUAD], F32, align_bytes=64)
-            nc.vector.transpose(
-                out=flipped[:].rearrange("p b w j -> p (b w j)"),
-                in_=x_tiles[m][:].rearrange("p b k -> p (b k)").bitcast(F32),
-            )
-            return flipped
-
-        def group_window(m, flipped):
-            xg = q_pool.tile([P, X_PASSES, P, PAIRS], F32, align_bytes=64)
+            words = x_tiles[m][:].bitcast(F32)
+            xt = psum.tile([P, X_PASSES, PAIRS, P], F32, tag="xt")
             for g in range(X_PASSES):
-                nc.scalar.copy(
-                    out=xg[:, g, :, :].rearrange("p (b j) u -> p b j u", j=QUAD),
-                    in_=flipped[:, :, g : K_BLOCKS : X_PASSES, :].rearrange("p b u j -> p b j u"),
-                )
+                for u in range(PAIRS):
+                    first = (g * PAIRS + u) * P
+                    nc.tensor.transpose(xt[:, g, u, :], words[:, first : first + P], ident_f32[:])
+            return xt
+
+        def group_window(xt):
+            xg = q_pool.tile([P, X_PASSES, P, PAIRS], F32, align_bytes=64)
+            nc.scalar.copy(out=xg[:], in_=xt[:].rearrange("p g u t -> p g t u"))
             return xg
 
         def quantise_window(m, xg):
@@ -201,7 +189,7 @@ def tile_localattention_pb_t_kernel(tc, x, Wv, bv, attn_band, Wo, bo, out):
             halves = []
             for h in range(D_HALVES):
                 cols = slice(h * N_TILE, (h + 1) * N_TILE)
-                o = out_psum.tile([P, N_TILE], F32, tag="o")
+                o = psum.tile([P, N_TILE], F32, tag="o")
                 nc.tensor.matmul_mx(
                     out=o[:],
                     lhsT=ctx_codes[:, tokens].bitcast(FP8X4),
@@ -219,17 +207,20 @@ def tile_localattention_pb_t_kernel(tc, x, Wv, bv, attn_band, Wo, bo, out):
             nc.vector.tensor_tensor(out=result[:, cols], in0=halves[h][:], in1=bo_all[:, cols], op=ADD)
 
         def prepare_wv():
-            nc.vector.transpose(
-                out=wv_flipped[:].rearrange("p b w j -> p (b w j)"),
-                in_=wv_raw[:].rearrange("p b k -> p (b k)").bitcast(F32),
-            )
+            half = E // 2
             for g in range(X_PASSES):
-                dst = wv_grouped[:, g, :, :].rearrange("p (b j) u -> p b j u", j=QUAD)
-                src = wv_flipped[:, :, g : K_BLOCKS : X_PASSES, :].rearrange("p b u j -> p b j u")
-                if g == 0:
-                    nc.scalar.copy(out=dst, in_=src)
-                else:
-                    nc.vector.tensor_copy(out=dst, in_=src)
+                for h in range(2):
+                    wt = psum.tile([P, PAIRS, half], F32, tag="o")
+                    for u in range(PAIRS):
+                        first = (g * (PAIRS) + u) * P
+                        for c in range(half // P):
+                            words = wv_raw[:, h * (half // P) + c, :].bitcast(F32)
+                            nc.tensor.transpose(wt[:, u, c * P : (c + 1) * P], words[:, first : first + P], ident_f32[:])
+                    dst = wv_grouped[:, g, h * half : (h + 1) * half, :]
+                    if h == 0:
+                        nc.scalar.copy(out=dst, in_=wt[:].rearrange("p u e -> p e u"))
+                    else:
+                        nc.vector.tensor_copy(out=dst, in_=wt[:].rearrange("p u e -> p e u"))
             for g in range(X_PASSES):
                 nc.vector.quantize_mx(
                     out=wv_codes[:, g, :].bitcast(FP8X4),
@@ -239,7 +230,7 @@ def tile_localattention_pb_t_kernel(tc, x, Wv, bv, attn_band, Wo, bo, out):
 
         def prepare_wo(q):
             cols = D // WO_PARTS
-            wt = out_psum.tile([P, PACK, cols], BF16, tag="o")
+            wt = psum.tile([P, PACK, cols], BF16, tag="o")
             for t in range(PACK):
                 for c in range(cols // P):
                     nc.tensor.transpose(
@@ -310,16 +301,18 @@ def tile_localattention_pb_t_kernel(tc, x, Wv, bv, attn_band, Wo, bo, out):
                 out=scratch[0:T].rearrange("(p r) -> p r", p=P), in_=weight_sums[:]
             )
 
-        def load_band():
-            for quad in range(P // QUAD):
-                row = quad * QUAD
+        def load_band(lo, hi):
+            count = hi - lo
+            for row, rows in BAND_ROWS:
                 col_lo = max(row - HALF, 0)
-                col_hi = min(row + QUAD + HALF, TOK)
-                start = Z_START + Z_PITCH * row + col_lo - row + HALF
-                src = scratch[start : start + N_WIN * Z_PITCH * WIN_STEP]
-                src = src.rearrange("(m y) -> m y", m=N_WIN)[:, 0 : QUAD * (Z_PITCH - 1)]
-                src = src.rearrange("m (r c) -> r m c", r=QUAD)[:, :, 0 : col_hi - col_lo]
-                nc.sync.dma_start(out=band_t[row : row + QUAD, :, col_lo:col_hi], in_=src)
+                col_hi = min(row + rows + HALF, TOK)
+                start = Z_START + Z_PITCH * (window_base(lo) + row) + col_lo - row + HALF
+                src = scratch[start : start + count * Z_PITCH * WIN_STEP]
+                src = src.rearrange("(m y) -> m y", m=count)[:, 0 : rows * (Z_PITCH - 1)]
+                src = src.rearrange("m (r c) -> r m c", r=rows)[:, :, 0 : col_hi - col_lo]
+                nc.sync.dma_start(out=band_t[row : row + rows, lo:hi, col_lo:col_hi], in_=src)
+
+        def load_sums():
             first = scratch[0:MAX_OUT].rearrange("(o y) -> o y", o=1)
             nc.sync.dma_start(out=band_t[TOK:P, 0, 0:MAX_OUT], in_=first)
             others = scratch[MAX_OUT : MAX_OUT + (N_WIN - 1) * WIN_STEP]
@@ -331,32 +324,31 @@ def tile_localattention_pb_t_kernel(tc, x, Wv, bv, attn_band, Wo, bo, out):
         nc.vector.memset(before_raw[:], 0.0)
         nc.vector.memset(after_raw[:], 0.0)
         nc.sync.dma_start(out=band_raw[:], in_=weights)
-        nc.sync.dma_start(out=before_raw[1:P, :, :], in_=weights[0 : P - 1, ROWS - HALF : ROWS, :])
-        nc.sync.dma_start(out=after_raw[0 : P - 1, :, :], in_=weights[1:P, 0:HALF, :])
-        for a in range(N_QUAD):
-            nc.sync.dma_start(
-                out=wv_raw[a * QUAD : (a + 1) * QUAD, :, :],
-                in_=Wv[:, a * K_QUAD : (a + 1) * K_QUAD].rearrange("(b j) k -> j b k", j=QUAD),
-            )
-        for m in range(2):
+        nc.scalar.dma_start(out=before_raw[1:P, :, :], in_=weights[0 : P - 1, ROWS - HALF : ROWS, :])
+        nc.scalar.dma_start(out=after_raw[0 : P - 1, :, :], in_=weights[1:P, 0:HALF, :])
+        nc.sync.dma_start(out=wv_raw[:], in_=Wv.rearrange("(c p) k -> p c k", p=P))
+        for m in range(3):
             load_window(m)
         nc.sync.dma_start(out=bv_rows[P - QUAD : P, :], in_=bv.partition_broadcast(QUAD))
         nc.sync.dma_start(out=wo_raw[:], in_=Wo.rearrange("(c p) k -> p c k", p=P))
-        for m in range(2, X_AHEAD):
+        for m in range(3, X_AHEAD):
             load_window(m)
-        nc.sync.dma_start(out=bo_all[:], in_=bo.partition_broadcast(P))
         nc.vector.memset(zero_rows[:], 0.0)
         nc.vector.memset(z_rows[:], 0.0)
         make_masks()
+        make_identity(nc, ident_f32[:])
         make_identity(nc, ident_bf16[:])
         nc.gpsimd.memset(band_t[:], 0.0)
         store_band_scratch()
-        load_band()
+        load_band(0, BAND_FIRST)
+        load_sums()
+        load_band(BAND_FIRST, N_WIN)
+        nc.sync.dma_start(out=bo_all[:], in_=bo.partition_broadcast(P))
         prepare_wv()
 
         previous = []
         blocks_done = 0
-        grouped = flipped = None
+        grouped = turned = None
         for step in range(N_WIN + LEAD + 4):
             mixing = step - 2 - LEAD
             mixed = min(max(mixing, 0), N_WIN)
@@ -366,31 +358,28 @@ def tile_localattention_pb_t_kernel(tc, x, Wv, bv, attn_band, Wo, bo, out):
                 load_window(step + X_AHEAD)
             for tb in blocks:
                 quantise_block(tb)
-            ct = mix_window(mixing) if 0 <= mixing < N_WIN else None
             if 0 <= step - 1 < N_WIN:
-                grouped = group_window(step - 1, flipped)
+                grouped = group_window(turned)
+            if step < N_WIN:
+                turned = transpose_window(step)
+            if WO_FIRST <= step < WO_FIRST + WO_PARTS:
+                prepare_wo(step - WO_FIRST)
+            ct = mix_window(mixing) if 0 <= mixing < N_WIN else None
             v0 = project_values(step - 2) if 0 <= step - 2 < N_WIN else None
             if ct is not None:
                 keep_context(mixing, ct)
             if v0 is not None:
                 keep_values(step - 2, v0)
             projected = [(tb, project_block(tb)) for tb in blocks]
-            results = []
             for tb, halves in previous:
                 result = o_pool.tile([P, D], F32)
-                add_bias(result, halves, 0)
-                results.append(result)
-            if step < N_WIN:
-                flipped = transpose_window(step)
-            for (tb, halves), result in zip(previous, results):
-                add_bias(result, halves, 1)
+                for h in range(D_HALVES):
+                    add_bias(result, halves, h)
                 nc.sync.dma_start(out=out_rows[tb * P : (tb + 1) * P, :], in_=result[:])
             if 0 <= step - 1 < N_WIN:
                 quantise_window(step - 1, grouped)
             previous = projected
-            if step < WO_PARTS:
-                prepare_wo(step)
-            if WO_PARTS <= step < WO_PARTS + D_HALVES:
-                quantise_wo(step - WO_PARTS)
+            if WO_FIRST + WO_PARTS <= step < WO_FIRST + WO_PARTS + D_HALVES:
+                quantise_wo(step - WO_FIRST - WO_PARTS)
             if step < N_V:
                 nc.vector.tensor_copy(out=v_tiles[step][P - QUAD : P, :], in_=bv_rows[P - QUAD : P, :])

from contextlib import ExitStack

import concourse.mybir as mybir
from concourse.masks import make_identity

F32 = mybir.dt.float32
BF16 = mybir.dt.bfloat16
U32 = mybir.dt.uint32
U8 = mybir.dt.uint8
FP8X4 = mybir.dt.float8_e4m3fn_x4
ADD = mybir.AluOpType.add
MULT = mybir.AluOpType.mult
MIN = mybir.AluOpType.min
NOT_EQUAL = mybir.AluOpType.not_equal
IS_GE = mybir.AluOpType.is_ge
AXIS_X = mybir.AxisListType.X

B, S, D, E, NW = 8, 512, 1024, 512, 11
HALF = NW // 2
T = B * S
P = 128
QUAD = 32
PACK = 4
K_PASS = P * PACK
X_PASSES = D // K_PASS
PAIRS = PACK // 2
N_TILE = 512
D_HALVES = D // N_TILE
ROWS = T // P
PARTS = P // B

TOK = P - 1
WIN_STEP = TOK - 2 * HALF
N_WIN = -(-(T - HALF) // WIN_STEP)
FIRST_OUT = [0] + [m * WIN_STEP + HALF for m in range(1, N_WIN)] + [T]
MAX_OUT = WIN_STEP + HALF

LEAD = 3
X_AHEAD = 6
N_V = LEAD + 3
WO_PARTS = 4
WO_FIRST = 1

Z_PITCH = QUAD + NW + HALF
BAND_ROWS = ((0, QUAD), (QUAD, QUAD), (2 * QUAD, QUAD), (3 * QUAD, QUAD // 2), (3 * QUAD + QUAD // 2, QUAD // 2 - 1))
BAND_FIRST = 8
SCRATCH_ROW = T - S
Z_START = T
Z_END = Z_START + T * Z_PITCH

FLOPS = 2 * T * D * E + 2 * T * NW * E + 2 * T * E * D


def window_base(m):
    return m * WIN_STEP


def tile_localattention_pb_t_kernel(tc, x, Wv, bv, attn_band, Wo, bo, out):
    nc = tc.nc
    x_rows = x.rearrange("b s d -> (b s) d")
    out_rows = out.rearrange("b s d -> (b s) d")
    scratch = out_rows[SCRATCH_ROW:T, :].rearrange("r d -> (r d)")

    with ExitStack() as stack:
        keep = stack.enter_context(tc.tile_pool(name="keep", bufs=1))
        x_pool = stack.enter_context(tc.tile_pool(name="x_pool", bufs=X_AHEAD + 2))
        q_pool = stack.enter_context(tc.tile_pool(name="q_pool", bufs=3))
        o_pool = stack.enter_context(tc.tile_pool(name="o_pool", bufs=4))
        psum = stack.enter_context(tc.psum_pool(name="psum", bufs=2))

        ident_f32 = keep.tile([P, P], F32)
        ident_bf16 = keep.tile([P, P], BF16)
        bv_rows = keep.tile([P, E], BF16)
        bo_all = keep.tile([P, D], BF16)
        wv_raw = keep.tile([P, E // P, D], BF16)
        wo_raw = keep.tile([P, D // P, E], BF16)
        wv_grouped = keep.tile([P, X_PASSES, E, PAIRS], F32, align_bytes=64)
        wo_grouped = keep.tile([P, D, PACK], BF16, align_bytes=64)
        wv_codes = keep.tile([P, X_PASSES, E], U32, align_bytes=64)
        wv_scales = keep.tile([P, X_PASSES, E], U8, align_bytes=64)
        wo_codes = keep.tile([P, D], U32, align_bytes=64)
        wo_scales = keep.tile([P, D], U8, align_bytes=64)
        band_raw = keep.tile([P, ROWS, NW], BF16)
        before_raw = keep.tile([P, HALF, NW], BF16)
        after_raw = keep.tile([P, HALF, NW], BF16)
        band_f32 = keep.tile([P, HALF + ROWS + HALF, NW], F32)
        not_first = keep.tile([P, B], F32)
        not_last = keep.tile([P, B], F32)
        not_first_part = keep.tile([P, 1], F32)
        not_last_part = keep.tile([P, 1], F32)
        first_mask = keep.tile([P, HALF, NW], F32)
        last_mask = keep.tile([P, HALF, NW], F32)
        weight_sums = keep.tile([P, ROWS], F32)
        z_rows = keep.tile([P, ROWS, Z_PITCH], F32)
        zero_rows = keep.tile([P, Z_PITCH], F32)
        band_t = keep.tile([P, N_WIN, P], F32)
        ctx_grouped = keep.tile([P, T, PACK], BF16, align_bytes=64)
        ctx_codes = keep.tile([P, T], U32, align_bytes=64)
        ctx_scales = keep.tile([P, T], U8, align_bytes=64)

        v_tiles = [keep.tile([P, E], F32, name="v%d" % n) for n in range(N_V)]

        x_tiles = {}
        x_code_tiles = {}

        def load_window(m):
            xw = x_pool.tile([P, D], BF16)
            rows = min(P, T - window_base(m))
            if rows < P:
                nc.gpsimd.memset(xw[:], 0.0)
            nc.sync.dma_start(out=xw[0:rows, :], in_=x_rows[window_base(m) : window_base(m) + rows, :])
            x_tiles[m] = xw

        def transpose_window(m):
            words = x_tiles[m][:].bitcast(F32)
            xt = psum.tile([P, X_PASSES, PAIRS, P], F32, tag="xt")
            for g in range(X_PASSES):
                for u in range(PAIRS):
                    first = (g * PAIRS + u) * P
                    nc.tensor.transpose(xt[:, g, u, :], words[:, first : first + P], ident_f32[:])
            return xt

        def group_window(xt):
            xg = q_pool.tile([P, X_PASSES, P, PAIRS], F32, align_bytes=64)
            nc.scalar.copy(out=xg[:], in_=xt[:].rearrange("p g u t -> p g t u"))
            return xg

        def quantise_window(m, xg):
            x_codes = q_pool.tile([P, X_PASSES, P], U32, align_bytes=64)
            x_scales = q_pool.tile([P, X_PASSES, P], U8, align_bytes=64)
            nc.vector.quantize_mx(
                out=x_codes[:].rearrange("p g t -> p (g t)").bitcast(FP8X4),
                scales=x_scales[:].rearrange("p g t -> p (g t)"),
                in_=xg[:].rearrange("p g t u -> p (g t u)").bitcast(BF16),
            )
            x_code_tiles[m] = (x_codes, x_scales)

        def project_values(m):
            x_codes, x_scales = x_code_tiles[m]
            v0 = psum.tile([P, E], F32, tag="v0")
            for g in range(X_PASSES):
                nc.tensor.matmul_mx(
                    out=v0[:],
                    lhsT=x_codes[:, g, :].bitcast(FP8X4),
                    lhsT_scale=x_scales[:, g, :],
                    rhs=wv_codes[:, g, :].bitcast(FP8X4),
                    rhs_scale=wv_scales[:, g, :],
                    start=(g == 0),
                    stop=(g == X_PASSES - 1),
                )
            return v0

        def keep_values(m, v0):
            nc.scalar.copy(out=v_tiles[m % N_V][0:TOK, :], in_=v0[0:TOK, :])

        def mix_window(m):
            first, last = FIRST_OUT[m], FIRST_OUT[m + 1]
            width = last - first
            col = first - window_base(m)
            ct = psum.tile([P, PACK, MAX_OUT], F32, tag="ct")
            for t in range(PACK):
                nc.tensor.matmul(
                    ct[:, t, 0:width],
                    lhsT=v_tiles[m % N_V][:, t * P : (t + 1) * P],
                    rhs=band_t[:, m, col : col + width],
                    start=True,
                    stop=True,
                )
            return ct

        def keep_context(m, ct):
            first, last = FIRST_OUT[m], FIRST_OUT[m + 1]
            width = last - first
            nc.scalar.copy(
                out=ctx_grouped[:, first:last, :],
                in_=ct[:, :, 0:width].rearrange("p t w -> p w t"),
            )

        def quantise_block(tb):
            tokens = slice(tb * P, (tb + 1) * P)
            nc.vector.quantize_mx(
                out=ctx_codes[:, tokens].bitcast(FP8X4),
                scales=ctx_scales[:, tokens],
                in_=ctx_grouped[:, tokens, :].rearrange("p w t -> p (w t)"),
            )

        def project_block(tb):
            tokens = slice(tb * P, (tb + 1) * P)
            halves = []
            for h in range(D_HALVES):
                cols = slice(h * N_TILE, (h + 1) * N_TILE)
                o = psum.tile([P, N_TILE], F32, tag="o")
                nc.tensor.matmul_mx(
                    out=o[:],
                    lhsT=ctx_codes[:, tokens].bitcast(FP8X4),
                    lhsT_scale=ctx_scales[:, tokens],
                    rhs=wo_codes[:, cols].bitcast(FP8X4),
                    rhs_scale=wo_scales[:, cols],
                    start=True,
                    stop=True,
                )
                halves.append(o)
            return halves

        def add_bias(result, halves, h):
            cols = slice(h * N_TILE, (h + 1) * N_TILE)
            nc.vector.tensor_tensor(out=result[:, cols], in0=halves[h][:], in1=bo_all[:, cols], op=ADD)

        def prepare_wv():
            half = E // 2
            for g in range(X_PASSES):
                for h in range(2):
                    wt = psum.tile([P, PAIRS, half], F32, tag="o")
                    for u in range(PAIRS):
                        first = (g * (PAIRS) + u) * P
                        for c in range(half // P):
                            words = wv_raw[:, h * (half // P) + c, :].bitcast(F32)
                            nc.tensor.transpose(wt[:, u, c * P : (c + 1) * P], words[:, first : first + P], ident_f32[:])
                    dst = wv_grouped[:, g, h * half : (h + 1) * half, :]
                    if h == 0:
                        nc.scalar.copy(out=dst, in_=wt[:].rearrange("p u e -> p e u"))
                    else:
                        nc.vector.tensor_copy(out=dst, in_=wt[:].rearrange("p u e -> p e u"))
            for g in range(X_PASSES):
                nc.vector.quantize_mx(
                    out=wv_codes[:, g, :].bitcast(FP8X4),
                    scales=wv_scales[:, g, :],
                    in_=wv_grouped[:, g, :, :].rearrange("p e u -> p (e u)").bitcast(BF16),
                )

        def prepare_wo(q):
            cols = D // WO_PARTS
            wt = psum.tile([P, PACK, cols], BF16, tag="o")
            for t in range(PACK):
                for c in range(cols // P):
                    nc.tensor.transpose(
                        wt[:, t, c * P : (c + 1) * P],
                        wo_raw[:, q * (cols // P) + c, t * P : (t + 1) * P],
                        ident_bf16[:],
                    )
            dst = wo_grouped[:, q * cols : (q + 1) * cols, :]
            if q % 2 == 0:
                nc.scalar.copy(out=dst, in_=wt[:].rearrange("p t d -> p d t"))
            else:
                nc.vector.tensor_copy(out=dst, in_=wt[:].rearrange("p t d -> p d t"))

        def quantise_wo(h):
            cols = slice(h * N_TILE, (h + 1) * N_TILE)
            nc.vector.quantize_mx(
                out=wo_codes[:, cols].bitcast(FP8X4),
                scales=wo_scales[:, cols],
                in_=wo_grouped[:, cols, :].rearrange("p d t -> p (d t)"),
            )

        def make_masks():
            for tile, part, edge in ((not_first, not_first_part, 0), (not_last, not_last_part, PARTS - 1)):
                nc.gpsimd.memset(tile[:], 1.0)
                nc.gpsimd.affine_select(
                    out=tile[:], in_=tile[:], pattern=[[-PARTS, B]],
                    compare_op=NOT_EQUAL, fill=0.0, base=-edge, channel_multiplier=1,
                )
                nc.vector.tensor_reduce(out=part[:], in_=tile[:], axis=AXIS_X, op=MIN)
            nc.gpsimd.memset(first_mask[:], 1.0)
            nc.gpsimd.affine_select(
                out=first_mask[:], in_=first_mask[:], pattern=[[1, HALF], [1, NW]],
                compare_op=IS_GE, fill=0.0, base=-HALF, channel_multiplier=0,
            )
            nc.gpsimd.memset(last_mask[:], 1.0)
            nc.gpsimd.affine_select(
                out=last_mask[:], in_=last_mask[:], pattern=[[-1, HALF], [-1, NW]],
                compare_op=IS_GE, fill=0.0, base=2 * HALF - 1, channel_multiplier=0,
            )
            nc.vector.tensor_scalar_max(out=first_mask[:], in0=first_mask[:], scalar1=not_first_part[:])
            nc.vector.tensor_scalar_max(out=last_mask[:], in0=last_mask[:], scalar1=not_last_part[:])

        def store_band_scratch():
            nc.vector.tensor_scalar_mul(out=band_f32[:, 0:HALF, :], in0=before_raw[:], scalar1=not_first_part[:])
            nc.vector.tensor_scalar_mul(
                out=band_f32[:, HALF + ROWS : HALF + ROWS + HALF, :], in0=after_raw[:], scalar1=not_last_part[:]
            )
            own = band_f32[:, HALF : HALF + ROWS, :]
            nc.scalar.copy(out=own[:, HALF : ROWS - HALF, :], in_=band_raw[:, HALF : ROWS - HALF, :])
            nc.vector.tensor_tensor(out=own[:, 0:HALF, :], in0=band_raw[:, 0:HALF, :], in1=first_mask[:], op=MULT)
            nc.vector.tensor_tensor(
                out=own[:, ROWS - HALF : ROWS, :], in0=band_raw[:, ROWS - HALF : ROWS, :], in1=last_mask[:], op=MULT
            )
            for d in range(NW):
                nc.vector.tensor_copy(
                    out=z_rows[:, :, d : d + 1], in_=band_f32[:, d : d + ROWS, NW - 1 - d : NW - d]
                )
            nc.scalar.dma_start(
                out=scratch[Z_START:Z_END].rearrange("(p x) -> p x", p=P),
                in_=z_rows[:].rearrange("p r c -> p (r c)"),
            )
            nc.scalar.dma_start(
                out=scratch[Z_END : Z_END + P * Z_PITCH].rearrange("(p c) -> p c", p=P),
                in_=zero_rows[:],
            )
            nc.vector.tensor_reduce(out=weight_sums[:], in_=own, axis=AXIS_X, op=ADD)
            nc.scalar.dma_start(
                out=scratch[0:T].rearrange("(p r) -> p r", p=P), in_=weight_sums[:]
            )

        def load_band(lo, hi):
            count = hi - lo
            for row, rows in BAND_ROWS:
                col_lo = max(row - HALF, 0)
                col_hi = min(row + rows + HALF, TOK)
                start = Z_START + Z_PITCH * (window_base(lo) + row) + col_lo - row + HALF
                src = scratch[start : start + count * Z_PITCH * WIN_STEP]
                src = src.rearrange("(m y) -> m y", m=count)[:, 0 : rows * (Z_PITCH - 1)]
                src = src.rearrange("m (r c) -> r m c", r=rows)[:, :, 0 : col_hi - col_lo]
                nc.sync.dma_start(out=band_t[row : row + rows, lo:hi, col_lo:col_hi], in_=src)

        def load_sums():
            first = scratch[0:MAX_OUT].rearrange("(o y) -> o y", o=1)
            nc.sync.dma_start(out=band_t[TOK:P, 0, 0:MAX_OUT], in_=first)
            others = scratch[MAX_OUT : MAX_OUT + (N_WIN - 1) * WIN_STEP]
            others = others.rearrange("(o m y) -> o m y", o=1, m=N_WIN - 1)
            nc.sync.dma_start(out=band_t[TOK:P, 1:N_WIN, HALF:MAX_OUT], in_=others)

        stack.enter_context(tc.manual_schedule())
        weights = attn_band.rearrange("b s o -> (b s o)").rearrange("(p r o) -> p r o", p=P, o=NW)
        nc.vector.memset(before_raw[:], 0.0)
        nc.vector.memset(after_raw[:], 0.0)
        nc.sync.dma_start(out=band_raw[:], in_=weights)
        nc.scalar.dma_start(out=before_raw[1:P, :, :], in_=weights[0 : P - 1, ROWS - HALF : ROWS, :])
        nc.scalar.dma_start(out=after_raw[0 : P - 1, :, :], in_=weights[1:P, 0:HALF, :])
        nc.sync.dma_start(out=wv_raw[:], in_=Wv.rearrange("(c p) k -> p c k", p=P))
        for m in range(3):
            load_window(m)
        nc.sync.dma_start(out=bv_rows[P - QUAD : P, :], in_=bv.partition_broadcast(QUAD))
        nc.sync.dma_start(out=wo_raw[:], in_=Wo.rearrange("(c p) k -> p c k", p=P))
        for m in range(3, X_AHEAD):
            load_window(m)
        nc.vector.memset(zero_rows[:], 0.0)
        nc.vector.memset(z_rows[:], 0.0)
        make_masks()
        make_identity(nc, ident_f32[:])
        make_identity(nc, ident_bf16[:])
        nc.gpsimd.memset(band_t[:], 0.0)
        store_band_scratch()
        load_band(0, BAND_FIRST)
        load_sums()
        load_band(BAND_FIRST, N_WIN)
        nc.sync.dma_start(out=bo_all[:], in_=bo.partition_broadcast(P))
        prepare_wv()

        previous = []
        blocks_done = 0
        grouped = turned = None
        for step in range(N_WIN + LEAD + 4):
            mixing = step - 2 - LEAD
            mixed = min(max(mixing, 0), N_WIN)
            blocks = list(range(blocks_done, FIRST_OUT[mixed] // P))
            blocks_done += len(blocks)
            if step + X_AHEAD < N_WIN:
                load_window(step + X_AHEAD)
            for tb in blocks:
                quantise_block(tb)
            if 0 <= step - 1 < N_WIN:
                grouped = group_window(turned)
            if step < N_WIN:
                turned = transpose_window(step)
            if WO_FIRST <= step < WO_FIRST + WO_PARTS:
                prepare_wo(step - WO_FIRST)
            ct = mix_window(mixing) if 0 <= mixing < N_WIN else None
            v0 = project_values(step - 2) if 0 <= step - 2 < N_WIN else None
            if ct is not None:
                keep_context(mixing, ct)
            if v0 is not None:
                keep_values(step - 2, v0)
            projected = [(tb, project_block(tb)) for tb in blocks]
            for tb, halves in previous:
                result = o_pool.tile([P, D], F32)
                for h in range(D_HALVES):
                    add_bias(result, halves, h)
                nc.sync.dma_start(out=out_rows[tb * P : (tb + 1) * P, :], in_=result[:])
            if 0 <= step - 1 < N_WIN:
                quantise_window(step - 1, grouped)
            previous = projected
            if WO_FIRST + WO_PARTS <= step < WO_FIRST + WO_PARTS + D_HALVES:
                quantise_wo(step - WO_FIRST - WO_PARTS)
            if step < N_V:
                nc.vector.tensor_copy(out=v_tiles[step][P - QUAD : P, :], in_=bv_rows[P - QUAD : P, :])
